import numpy as np
import ml_dtypes

BF16 = ml_dtypes.bfloat16


def bf(x):
    return np.asarray(x, np.float32).astype(BF16)


def f32(x):
    return np.asarray(x, np.float32)


def f64(x):
    return np.asarray(x).astype(np.float64)


def striped(idx):
    return np.tile(idx.reshape(-1, 16).T, (8, 1))


D, S, M, N = 128, 512, 512, 128


def setup_inputs():
    return {"table": bf(0.1 * np.random.standard_normal((D, S))), "feat": bf(np.abs(np.random.standard_normal((D, M)))), "offs": striped(np.random.permutation(S)[:N])}


def reference(table, feat, offs):
    idx = offs[:16].T.reshape(-1)
    z = f64(feat).T @ f64(table)[:, idx]
    return 1.0 / (1.0 + np.exp(-z))

@@ -1,0 +1,36 @@
+import concourse.mybir as mybir
+
+BF16, F32, U16 = mybir.dt.bfloat16, mybir.dt.float32, mybir.dt.uint16
+SIGMOID = mybir.ActivationFunctionType.Sigmoid
+
+P = 128
+PLACES = 512
+OBJECTS = 128
+BLOCKS = PLACES // P
+
+FLOPS = 2 * P * PLACES * OBJECTS
+
+
+def tile_diceloss_kernel(tc, table, feat, offs, out):
+    nc = tc.nc
+    with (
+        tc.tile_pool(name="held", bufs=1) as held,
+        tc.tile_pool(name="results", bufs=BLOCKS) as results,
+        tc.psum_pool(name="psum", bufs=BLOCKS) as psum,
+    ):
+        offsets = held.tile([P, OBJECTS // 16], U16, name="offsets")
+        nc.sync.dma_start(offsets[:], offs)
+        filters = held.tile([P, PLACES], BF16, name="filters")
+        nc.sync.dma_start(filters[:], table)
+        features = held.tile([P, PLACES], BF16, name="features")
+        nc.scalar.dma_start(features[:], feat)
+
+        for b in range(BLOCKS):
+            places = slice(b * P, (b + 1) * P)
+            logits = psum.tile([P, OBJECTS], F32, name="logits")
+            nc.tensor.matmul(
+                logits[:], features[:, places], filters[:].indirect(offsets[:]), start=True, stop=True
+            )
+            values = results.tile([P, OBJECTS], F32, name="values")
+            nc.scalar.activation(values[:], logits[:], SIGMOID)
+            nc.sync.dma_start(out[places, :], values[:])

@@ -10,6 +10,8 @@ BLOCKS = PLACES // P
 
 FLOPS = 2 * P * PLACES * OBJECTS
 
+WARMING_MATMULS = 4
+
 
 def tile_diceloss_kernel(tc, table, feat, offs, out):
     nc = tc.nc
@@ -17,6 +19,7 @@ def tile_diceloss_kernel(tc, table, feat, offs, out):
         tc.tile_pool(name="held", bufs=1) as held,
         tc.tile_pool(name="results", bufs=BLOCKS) as results,
         tc.psum_pool(name="psum", bufs=BLOCKS) as psum,
+        tc.psum_pool(name="idle", bufs=1) as idle,
     ):
         offsets = held.tile([P, OBJECTS // 16], U16, name="offsets")
         nc.sync.dma_start(offsets[:], offs)
@@ -24,6 +27,12 @@ def tile_diceloss_kernel(tc, table, feat, offs, out):
         nc.sync.dma_start(filters[:], table)
         features = held.tile([P, PLACES], BF16, name="features")
         nc.scalar.dma_start(features[:], feat)
+
+        zeros = held.tile([P, PLACES], BF16, name="zeros")
+        nc.vector.memset(zeros[:], 0.0)
+        unread = idle.tile([P, PLACES], F32, name="unread")
+        for i in range(WARMING_MATMULS):
+            nc.tensor.matmul(unread[:], zeros[:, 0:P], zeros[:], start=True, stop=True)
 
         for b in range(BLOCKS):
             places = slice(b * P, (b + 1) * P)

@@ -10,8 +10,6 @@ BLOCKS = PLACES // P
 
 FLOPS = 2 * P * PLACES * OBJECTS
 
-WARMING_MATMULS = 4
-
 
 def tile_diceloss_kernel(tc, table, feat, offs, out):
     nc = tc.nc
@@ -19,26 +17,22 @@ def tile_diceloss_kernel(tc, table, feat, offs, out):
         tc.tile_pool(name="held", bufs=1) as held,
         tc.tile_pool(name="results", bufs=BLOCKS) as results,
         tc.psum_pool(name="psum", bufs=BLOCKS) as psum,
-        tc.psum_pool(name="idle", bufs=1) as idle,
     ):
         offsets = held.tile([P, OBJECTS // 16], U16, name="offsets")
         nc.sync.dma_start(offsets[:], offs)
         filters = held.tile([P, PLACES], BF16, name="filters")
         nc.sync.dma_start(filters[:], table)
-        features = held.tile([P, PLACES], BF16, name="features")
-        nc.scalar.dma_start(features[:], feat)
-
-        zeros = held.tile([P, PLACES], BF16, name="zeros")
-        nc.vector.memset(zeros[:], 0.0)
-        unread = idle.tile([P, PLACES], F32, name="unread")
-        for i in range(WARMING_MATMULS):
-            nc.tensor.matmul(unread[:], zeros[:, 0:P], zeros[:], start=True, stop=True)
+        features = []
+        for b in range(BLOCKS):
+            block = held.tile([P, P], BF16, name=f"features{b}")
+            nc.sync.dma_start(block[:], feat[:, b * P : (b + 1) * P])
+            features.append(block)
 
         for b in range(BLOCKS):
             places = slice(b * P, (b + 1) * P)
             logits = psum.tile([P, OBJECTS], F32, name="logits")
             nc.tensor.matmul(
-                logits[:], features[:, places], filters[:].indirect(offsets[:]), start=True, stop=True
+                logits[:], features[b][:], filters[:].indirect(offsets[:]), start=True, stop=True
             )
             values = results.tile([P, OBJECTS], F32, name="values")
             nc.scalar.activation(values[:], logits[:], SIGMOID)

@@ -22,17 +22,18 @@ def tile_diceloss_kernel(tc, table, feat, offs, out):
         nc.sync.dma_start(offsets[:], offs)
         filters = held.tile([P, PLACES], BF16, name="filters")
         nc.sync.dma_start(filters[:], table)
+        HALF = PLACES // 2
         features = []
-        for b in range(BLOCKS):
-            block = held.tile([P, P], BF16, name=f"features{b}")
-            nc.sync.dma_start(block[:], feat[:, b * P : (b + 1) * P])
-            features.append(block)
+        for h in range(2):
+            half = held.tile([P, HALF], BF16, name=f"features{h}")
+            nc.sync.dma_start(half[:], feat[:, h * HALF : (h + 1) * HALF])
+            features.extend([half[:, 0:P], half[:, P:HALF]])
 
         for b in range(BLOCKS):
             places = slice(b * P, (b + 1) * P)
             logits = psum.tile([P, OBJECTS], F32, name="logits")
             nc.tensor.matmul(
-                logits[:], features[b][:], filters[:].indirect(offsets[:]), start=True, stop=True
+                logits[:], features[b], filters[:].indirect(offsets[:]), start=True, stop=True
             )
             values = results.tile([P, OBJECTS], F32, name="values")
             nc.scalar.activation(values[:], logits[:], SIGMOID)

@@ -18,10 +18,10 @@ def tile_diceloss_kernel(tc, table, feat, offs, out):
         tc.tile_pool(name="results", bufs=BLOCKS) as results,
         tc.psum_pool(name="psum", bufs=BLOCKS) as psum,
     ):
-        offsets = held.tile([P, OBJECTS // 16], U16, name="offsets")
-        nc.sync.dma_start(offsets[:], offs)
         filters = held.tile([P, PLACES], BF16, name="filters")
         nc.sync.dma_start(filters[:], table)
+        offsets = held.tile([P, OBJECTS // 16], U16, name="offsets")
+        nc.sync.dma_start(offsets[:], offs)
         HALF = PLACES // 2
         features = []
         for h in range(2):

@@ -18,16 +18,15 @@ def tile_diceloss_kernel(tc, table, feat, offs, out):
         tc.tile_pool(name="results", bufs=BLOCKS) as results,
         tc.psum_pool(name="psum", bufs=BLOCKS) as psum,
     ):
+        HALF = PLACES // 2
         filters = held.tile([P, PLACES], BF16, name="filters")
         nc.sync.dma_start(filters[:], table)
+        halves = [held.tile([P, HALF], BF16, name=f"features{h}") for h in range(2)]
+        nc.sync.dma_start(halves[0][:], feat[:, 0:HALF])
         offsets = held.tile([P, OBJECTS // 16], U16, name="offsets")
         nc.sync.dma_start(offsets[:], offs)
-        HALF = PLACES // 2
-        features = []
-        for h in range(2):
-            half = held.tile([P, HALF], BF16, name=f"features{h}")
-            nc.sync.dma_start(half[:], feat[:, h * HALF : (h + 1) * HALF])
-            features.extend([half[:, 0:P], half[:, P:HALF]])
+        nc.sync.dma_start(halves[1][:], feat[:, HALF:PLACES])
+        features = [half[:, c : c + P] for half in halves for c in (0, P)]
 
         for b in range(BLOCKS):
             places = slice(b * P, (b + 1) * P)

import concourse.mybir as mybir

BF16, F32, U16 = mybir.dt.bfloat16, mybir.dt.float32, mybir.dt.uint16
SIGMOID = mybir.ActivationFunctionType.Sigmoid

P = 128
PLACES = 512
OBJECTS = 128
BLOCKS = PLACES // P

FLOPS = 2 * P * PLACES * OBJECTS


def tile_diceloss_kernel(tc, table, feat, offs, out):
    nc = tc.nc
    with (
        tc.tile_pool(name="held", bufs=1) as held,
        tc.tile_pool(name="results", bufs=BLOCKS) as results,
        tc.psum_pool(name="psum", bufs=BLOCKS) as psum,
    ):
        HALF = PLACES // 2
        filters = held.tile([P, PLACES], BF16, name="filters")
        nc.sync.dma_start(filters[:], table)
        halves = [held.tile([P, HALF], BF16, name=f"features{h}") for h in range(2)]
        nc.sync.dma_start(halves[0][:], feat[:, 0:HALF])
        offsets = held.tile([P, OBJECTS // 16], U16, name="offsets")
        nc.sync.dma_start(offsets[:], offs)
        nc.sync.dma_start(halves[1][:], feat[:, HALF:PLACES])
        features = [half[:, c : c + P] for half in halves for c in (0, P)]

        for b in range(BLOCKS):
            places = slice(b * P, (b + 1) * P)
            logits = psum.tile([P, OBJECTS], F32, name="logits")
            nc.tensor.matmul(
                logits[:], features[b], filters[:].indirect(offsets[:]), start=True, stop=True
            )
            values = results.tile([P, OBJECTS], F32, name="values")
            nc.scalar.activation(values[:], logits[:], SIGMOID)
            nc.sync.dma_start(out[places, :], values[:])
